import numpy as np
import ml_dtypes


def mxq(x, axis, fmt="e4m3"):
    dtype, down = {"e4m3": (ml_dtypes.float8_e4m3fn, 7), "e5m2": (ml_dtypes.float8_e5m2, 14)}[fmt]
    v = np.moveaxis(np.asarray(x, np.float32).astype(ml_dtypes.bfloat16).astype(np.float64), axis, -1)
    blocks = v.reshape(v.shape[:-1] + (-1, 32))
    amax = np.abs(blocks).max(-1, keepdims=True)
    byte = np.maximum(np.where(amax > 0, np.frexp(amax)[1] - 1 + 127, 0) - down, 1)
    scale = np.exp2(byte - 127.0)
    codes = (blocks / scale).astype(np.float32).astype(dtype).astype(np.float64)
    return np.moveaxis((codes * scale).reshape(v.shape), -1, axis)


WIDE = False


def mx_kscale(k):
    if not WIDE:
        return np.ones(k)
    levels = np.array([20, -20, 10, -10, 0])
    a = np.random.permutation(np.resize(levels, k // 512 * 4)).reshape(k // 512, 4)
    idx = np.arange(k)
    return np.exp2(a[idx // 512, idx % 128 // 32])


BF16 = ml_dtypes.bfloat16


def bf(x):
    return np.asarray(x, np.float32).astype(BF16)


def f64(x):
    return np.asarray(x).astype(np.float64)


B, I, O, G, P = 16384, 128, 512, 2, 2
L = G + P
SCALE_SPLINE = 1.0


def setup_inputs():
    u = mx_kscale(O)
    x = np.random.uniform(-1.0, 1.0, (B, I))
    sw = np.random.standard_normal((O, I, L)) * 2.0 / np.sqrt(I) / u[:, None, None]
    bw = np.random.standard_normal((O, I)) * 1.0 / np.sqrt(I) / u[:, None]
    g = np.random.standard_normal((B, O)) * np.exp2(np.random.randint(-12, 1, (B, 1))) * u
    return {"x": bf(x),
            "base_weight": bf(bw),
            "spline_weight": bf(sw),
            "grid": bf(np.arange(-P, G + P + 1) * (2.0 / G) - 1.0),
            "grad_out": bf(g)}


def b_spline_basis(x, grid, k):
    xe = x[..., None]
    basis = ((xe >= grid[:-1]) & (xe < grid[1:])).astype(np.float64)
    for d in range(1, k + 1):
        left_denom = grid[d:-1] - grid[:-(d + 1)]
        right_denom = grid[d + 1:] - grid[1:-d]
        left_denom = np.where(left_denom > 0, left_denom, 1.0)
        right_denom = np.where(right_denom > 0, right_denom, 1.0)
        basis = ((xe - grid[:-(d + 1)]) / left_denom * basis[..., :-1]
                 + (grid[d + 1:] - xe) / right_denom * basis[..., 1:])
    return basis


def b_spline_basis_deriv(x, grid, k):
    low = b_spline_basis(x, grid, k - 1)
    left_denom = grid[k:-1] - grid[:-(k + 1)]
    right_denom = grid[k + 1:] - grid[1:-k]
    return k * (low[..., :-1] / left_denom - low[..., 1:] / right_denom)


def reference(x, base_weight, spline_weight, grid, grad_out):
    x, base_weight, spline_weight, grid = f64(x), f64(base_weight), f64(spline_weight), f64(grid)
    gq = mxq(f64(grad_out), 1, "e5m2")
    base = gq @ mxq(base_weight, 0, "e4m3")
    t = gq @ mxq(spline_weight.reshape(O, I * L), 0, "e4m3")
    dbasis = b_spline_basis_deriv(x, grid, P)
    return base + SCALE_SPLINE * (t.reshape(B, I, L) * dbasis).sum(-1)

@@ -1,0 +1,189 @@
+import concourse.mybir as mybir
+from concourse.masks import make_identity
+
+F32 = mybir.dt.float32
+BF16 = mybir.dt.bfloat16
+U32 = mybir.dt.uint32
+U8 = mybir.dt.uint8
+E4M3_X4 = mybir.dt.float8_e4m3fn_x4
+E5M2_X4 = mybir.dt.float8_e5m2_x4
+ALU = mybir.AluOpType
+ACT = mybir.ActivationFunctionType
+
+P = 128
+PACK = 4
+TOKENS = 16384
+OUT_F = 512
+IN_F = 128
+BASES = 4
+HATS = BASES + 1
+BANK = 512
+HALF = OUT_F // 2
+TILES = 4
+CHUNK = P * TILES
+N_CHUNKS = TOKENS // CHUNK
+
+FLOPS = 2 * TOKENS * OUT_F * (IN_F + IN_F * BASES)
+
+
+def load_weight_rows(nc, raw, weight):
+    for u in range(2):
+        nc.scalar.dma_start(
+            out=raw[:, 2 * u : 2 * u + 2, :],
+            in_=weight[HALF * u : HALF * (u + 1), :].rearrange("(p e) c -> p e c", e=2),
+        )
+
+
+def tile_kanlayer_t_kernel(tc, x, base_weight, spline_weight, grid, grad_out, out):
+    nc = tc.nc
+    with (
+        tc.tile_pool(name="keep", bufs=1) as keep,
+        tc.tile_pool(name="loads", bufs=4) as loads,
+        tc.tile_pool(name="work", bufs=3) as work,
+        tc.tile_pool(name="stores", bufs=3) as stores,
+        tc.psum_pool(name="psum_t", bufs=2) as psum_t,
+        tc.psum_pool(name="psum_mx", bufs=3) as psum_mx,
+    ):
+        raw_sw = keep.tile([P, PACK, BASES * IN_F], BF16)
+        load_weight_rows(nc, raw_sw, spline_weight.rearrange("o i l -> o (i l)"))
+        raw_bw = keep.tile([P, PACK, IN_F], BF16)
+        load_weight_rows(nc, raw_bw, base_weight)
+        by_basis = raw_sw[:].rearrange("p k (i l) -> p l i k", l=BASES)
+
+        plus_bf = keep.tile([P, 2 * BASES, IN_F, PACK], BF16, align_bytes=64)
+        nc.vector.memset(plus_bf[:, 0, :, :], 0.0)
+        nc.vector.memset(plus_bf[:, BASES + 2 :, :, :], 0.0)
+        nc.vector.tensor_copy(out=plus_bf[:, 1 : BASES + 1, :, :], in_=by_basis)
+        nc.vector.tensor_copy(
+            out=plus_bf[:, BASES + 1, :, :], in_=raw_bw[:].rearrange("p k i -> p i k")
+        )
+        minus_bf = keep.tile([P, BASES, IN_F, PACK], BF16, align_bytes=64)
+        nc.vector.tensor_scalar(
+            out=minus_bf[:], in0=by_basis, scalar1=-1.0, scalar2=None, op0=ALU.mult
+        )
+
+        plus_codes = keep.tile([P, 2 * BANK], U32, align_bytes=64)
+        plus_scales = keep.tile([P, 2 * BANK], U8, align_bytes=64)
+        nc.vector.quantize_mx(
+            out=plus_codes[:].bitcast(E4M3_X4),
+            scales=plus_scales[:],
+            in_=plus_bf[:].rearrange("p a i k -> p (a i k)"),
+        )
+        minus_codes = keep.tile([P, BANK], U32, align_bytes=64)
+        minus_scales = keep.tile([P, BANK], U8, align_bytes=64)
+        nc.vector.quantize_mx(
+            out=minus_codes[:].bitcast(E4M3_X4),
+            scales=minus_scales[:],
+            in_=minus_bf[:].rearrange("p a i k -> p (a i k)"),
+        )
+
+        ident = keep.tile([P, P], F32)
+        make_identity(nc, ident[:])
+        grid_bf = keep.tile([P, HATS + 2], BF16)
+        nc.sync.dma_start(out=grid_bf[:], in_=grid.partition_broadcast(P))
+        minus_centre = keep.tile([P, HATS], F32)
+        nc.vector.tensor_scalar(
+            out=minus_centre[:], in0=grid_bf[:, 1 : HATS + 1], scalar1=-1.0, scalar2=None, op0=ALU.mult
+        )
+
+        g_rows = grad_out.rearrange("(c p t) o -> c p (t o)", p=P, t=TILES)
+        x_rows = x.rearrange("(c p t) i -> c p (t i)", p=P, t=TILES)
+        out_rows = out.rearrange("(c p t) i -> c p (t i)", p=P, t=TILES)
+
+        for c in range(N_CHUNKS):
+            g_sb = loads.tile([P, TILES * OUT_F], BF16)
+            nc.sync.dma_start(out=g_sb[:], in_=g_rows[c])
+            x_sb = loads.tile([P, TILES, IN_F], BF16)
+            nc.sync.dma_start(out=x_sb[:].rearrange("p t i -> p (t i)"), in_=x_rows[c])
+
+            g_words = g_sb[:].bitcast(F32)
+            g_bf = work.tile([P, TILES * OUT_F], BF16, align_bytes=64)
+            g_pairs = g_bf[:].bitcast(F32).rearrange("p (t r u) -> p t r u", r=P, u=2)
+            for pair in range(TILES // 2):
+                g_t = psum_t.tile([P, 4, P], F32)
+                for a in range(2):
+                    for u in range(2):
+                        first = ((2 * pair + a) * 2 + u) * P
+                        nc.tensor.transpose(
+                            g_t[:, 2 * a + u, :], g_words[:, first : first + P], ident[:]
+                        )
+                nc.scalar.copy(
+                    out=g_pairs[:, 2 * pair : 2 * pair + 2, :, :],
+                    in_=g_t[:].rearrange("p (a u) r -> p a r u", u=2),
+                )
+            g_codes = work.tile([P, TILES * P], U32, align_bytes=64)
+            g_scales = work.tile([P, TILES * P], U8, align_bytes=64)
+            nc.vector.quantize_mx(out=g_codes[:].bitcast(E5M2_X4), scales=g_scales[:], in_=g_bf[:])
+
+            dist = work.tile([P, TILES, HATS, IN_F], F32)
+            for j in range(HATS):
+                nc.scalar.activation(
+                    out=dist[:, :, j, :],
+                    in_=x_sb[:],
+                    func=ACT.Abs,
+                    bias=minus_centre[:, j : j + 1],
+                    scale=1.0,
+                )
+
+            prod = work.tile([P, TILES, HATS, IN_F], F32)
+            last = work.tile([P, TILES, IN_F], F32)
+            for t in range(TILES):
+                tokens = slice(t * P, (t + 1) * P)
+                g_tile = g_codes[:, tokens].bitcast(E5M2_X4)
+                g_tile_scales = g_scales[:, tokens]
+                steps = psum_mx.tile([P, BANK], F32)
+                nc.tensor.matmul_mx(
+                    out=steps[:],
+                    lhsT=g_tile,
+                    lhsT_scale=g_tile_scales,
+                    rhs=plus_codes[:, 0:BANK].bitcast(E4M3_X4),
+                    rhs_scale=plus_scales[:, 0:BANK],
+                    start=True,
+                    stop=False,
+                )
+                nc.tensor.matmul_mx(
+                    out=steps[:],
+                    lhsT=g_tile,
+                    lhsT_scale=g_tile_scales,
+                    rhs=minus_codes[:].bitcast(E4M3_X4),
+                    rhs_scale=minus_scales[:],
+                    start=False,
+                    stop=True,
+                )
+                rest = psum_mx.tile([P, BANK], F32)
+                nc.tensor.matmul_mx(
+                    out=rest[:],
+                    lhsT=g_tile,
+                    lhsT_scale=g_tile_scales,
+                    rhs=plus_codes[:, BANK : 2 * BANK].bitcast(E4M3_X4),
+                    rhs_scale=plus_scales[:, BANK : 2 * BANK],
+                    start=True,
+                    stop=True,
+                )
+                nc.vector.scalar_tensor_tensor(
+                    out=prod[:, t, BASES, :],
+                    in0=dist[:, t, BASES, :],
+                    scalar=1.0,
+                    in1=rest[:, 0:IN_F],
+                    op0=ALU.min,
+                    op1=ALU.mult,
+                )
+                nc.vector.scalar_tensor_tensor(
+                    out=prod[:, t, 0:BASES, :].rearrange("p j i -> p (j i)"),
+                    in0=dist[:, t, 0:BASES, :].rearrange("p j i -> p (j i)"),
+                    scalar=1.0,
+                    in1=steps[:],
+                    op0=ALU.min,
+                    op1=ALU.mult,
+                )
+                nc.vector.tensor_tensor(
+                    out=last[:, t, :], in0=prod[:, t, BASES, :], in1=rest[:, IN_F : 2 * IN_F], op=ALU.add
+                )
+
+            two = work.tile([P, TILES, 2, IN_F], F32)
+            nc.gpsimd.tensor_tensor(out=two[:], in0=prod[:, :, 0:2, :], in1=prod[:, :, 2:4, :], op=ALU.add)
+            four = work.tile([P, TILES, IN_F], F32)
+            nc.gpsimd.tensor_tensor(out=four[:], in0=two[:, :, 0, :], in1=two[:, :, 1, :], op=ALU.add)
+            out_sb = stores.tile([P, TILES, IN_F], F32)
+            nc.vector.tensor_tensor(out=out_sb[:], in0=four[:], in1=last[:], op=ALU.add)
+            nc.sync.dma_start(out=out_rows[c], in_=out_sb[:].rearrange("p t i -> p (t i)"))

@@ -22,6 +22,7 @@ HALF = OUT_F // 2
 TILES = 4
 CHUNK = P * TILES
 N_CHUNKS = TOKENS // CHUNK
+LOOKAHEAD = 3
 
 FLOPS = 2 * TOKENS * OUT_F * (IN_F + IN_F * BASES)
 
@@ -38,11 +39,12 @@ def tile_kanlayer_t_kernel(tc, x, base_weight, spline_weight, grid, grad_out, ou
     nc = tc.nc
     with (
         tc.tile_pool(name="keep", bufs=1) as keep,
-        tc.tile_pool(name="loads", bufs=4) as loads,
-        tc.tile_pool(name="work", bufs=3) as work,
+        tc.tile_pool(name="loads", bufs=LOOKAHEAD + 1) as loads,
+        tc.tile_pool(name="work", bufs=2) as work,
         tc.tile_pool(name="stores", bufs=3) as stores,
         tc.psum_pool(name="psum_t", bufs=2) as psum_t,
         tc.psum_pool(name="psum_mx", bufs=3) as psum_mx,
+        tc.manual_schedule(),
     ):
         raw_sw = keep.tile([P, PACK, BASES * IN_F], BF16)
         load_weight_rows(nc, raw_sw, spline_weight.rearrange("o i l -> o (i l)"))
@@ -90,17 +92,21 @@ def tile_kanlayer_t_kernel(tc, x, base_weight, spline_weight, grid, grad_out, ou
         x_rows = x.rearrange("(c p t) i -> c p (t i)", p=P, t=TILES)
         out_rows = out.rearrange("(c p t) i -> c p (t i)", p=P, t=TILES)
 
-        for c in range(N_CHUNKS):
-            g_sb = loads.tile([P, TILES * OUT_F], BF16)
-            nc.sync.dma_start(out=g_sb[:], in_=g_rows[c])
-            x_sb = loads.tile([P, TILES, IN_F], BF16)
-            nc.sync.dma_start(out=x_sb[:].rearrange("p t i -> p (t i)"), in_=x_rows[c])
 
-            g_words = g_sb[:].bitcast(F32)
-            g_bf = work.tile([P, TILES * OUT_F], BF16, align_bytes=64)
+        g_sb, x_sb, g_codes, g_scales, dist, prod, last, four = {}, {}, {}, {}, {}, {}, {}, {}
+
+        def load(c):
+            g_sb[c] = loads.tile([P, TILES * OUT_F], BF16, name="g_sb")
+            nc.sync.dma_start(out=g_sb[c][:], in_=g_rows[c])
+            x_sb[c] = loads.tile([P, TILES, IN_F], BF16, name="x_sb")
+            nc.sync.dma_start(out=x_sb[c][:].rearrange("p t i -> p (t i)"), in_=x_rows[c])
+
+        def transpose_and_measure(c):
+            g_words = g_sb[c][:].bitcast(F32)
+            g_bf = work.tile([P, TILES * OUT_F], BF16, align_bytes=64, name="g_bf")
             g_pairs = g_bf[:].bitcast(F32).rearrange("p (t r u) -> p t r u", r=P, u=2)
             for pair in range(TILES // 2):
-                g_t = psum_t.tile([P, 4, P], F32)
+                g_t = psum_t.tile([P, 4, P], F32, name="g_t")
                 for a in range(2):
                     for u in range(2):
                         first = ((2 * pair + a) * 2 + u) * P
@@ -111,79 +117,108 @@ def tile_kanlayer_t_kernel(tc, x, base_weight, spline_weight, grid, grad_out, ou
                     out=g_pairs[:, 2 * pair : 2 * pair + 2, :, :],
                     in_=g_t[:].rearrange("p (a u) r -> p a r u", u=2),
                 )
-            g_codes = work.tile([P, TILES * P], U32, align_bytes=64)
-            g_scales = work.tile([P, TILES * P], U8, align_bytes=64)
-            nc.vector.quantize_mx(out=g_codes[:].bitcast(E5M2_X4), scales=g_scales[:], in_=g_bf[:])
-
-            dist = work.tile([P, TILES, HATS, IN_F], F32)
+            dist[c] = work.tile([P, TILES, HATS, IN_F], F32, name="dist")
             for j in range(HATS):
                 nc.scalar.activation(
-                    out=dist[:, :, j, :],
-                    in_=x_sb[:],
+                    out=dist[c][:, :, j, :],
+                    in_=x_sb[c][:],
                     func=ACT.Abs,
                     bias=minus_centre[:, j : j + 1],
                     scale=1.0,
                 )
+            return g_bf
 
-            prod = work.tile([P, TILES, HATS, IN_F], F32)
-            last = work.tile([P, TILES, IN_F], F32)
-            for t in range(TILES):
-                tokens = slice(t * P, (t + 1) * P)
-                g_tile = g_codes[:, tokens].bitcast(E5M2_X4)
-                g_tile_scales = g_scales[:, tokens]
-                steps = psum_mx.tile([P, BANK], F32)
-                nc.tensor.matmul_mx(
-                    out=steps[:],
-                    lhsT=g_tile,
-                    lhsT_scale=g_tile_scales,
-                    rhs=plus_codes[:, 0:BANK].bitcast(E4M3_X4),
-                    rhs_scale=plus_scales[:, 0:BANK],
-                    start=True,
-                    stop=False,
-                )
-                nc.tensor.matmul_mx(
-                    out=steps[:],
-                    lhsT=g_tile,
-                    lhsT_scale=g_tile_scales,
-                    rhs=minus_codes[:].bitcast(E4M3_X4),
-                    rhs_scale=minus_scales[:],
-                    start=False,
-                    stop=True,
-                )
-                rest = psum_mx.tile([P, BANK], F32)
-                nc.tensor.matmul_mx(
-                    out=rest[:],
-                    lhsT=g_tile,
-                    lhsT_scale=g_tile_scales,
-                    rhs=plus_codes[:, BANK : 2 * BANK].bitcast(E4M3_X4),
-                    rhs_scale=plus_scales[:, BANK : 2 * BANK],
-                    start=True,
-                    stop=True,
-                )
-                nc.vector.scalar_tensor_tensor(
-                    out=prod[:, t, BASES, :],
-                    in0=dist[:, t, BASES, :],
-                    scalar=1.0,
-                    in1=rest[:, 0:IN_F],
-                    op0=ALU.min,
-                    op1=ALU.mult,
-                )
-                nc.vector.scalar_tensor_tensor(
-                    out=prod[:, t, 0:BASES, :].rearrange("p j i -> p (j i)"),
-                    in0=dist[:, t, 0:BASES, :].rearrange("p j i -> p (j i)"),
-                    scalar=1.0,
-                    in1=steps[:],
-                    op0=ALU.min,
-                    op1=ALU.mult,
-                )
-                nc.vector.tensor_tensor(
-                    out=last[:, t, :], in0=prod[:, t, BASES, :], in1=rest[:, IN_F : 2 * IN_F], op=ALU.add
-                )
+        def quantise(c, g_bf):
+            g_codes[c] = work.tile([P, TILES * P], U32, align_bytes=64, name="g_codes")
+            g_scales[c] = work.tile([P, TILES * P], U8, align_bytes=64, name="g_scales")
+            nc.vector.quantize_mx(
+                out=g_codes[c][:].bitcast(E5M2_X4), scales=g_scales[c][:], in_=g_bf[:]
+            )
 
-            two = work.tile([P, TILES, 2, IN_F], F32)
-            nc.gpsimd.tensor_tensor(out=two[:], in0=prod[:, :, 0:2, :], in1=prod[:, :, 2:4, :], op=ALU.add)
-            four = work.tile([P, TILES, IN_F], F32)
-            nc.gpsimd.tensor_tensor(out=four[:], in0=two[:, :, 0, :], in1=two[:, :, 1, :], op=ALU.add)
-            out_sb = stores.tile([P, TILES, IN_F], F32)
-            nc.vector.tensor_tensor(out=out_sb[:], in0=four[:], in1=last[:], op=ALU.add)
+        def multiply(c, t):
+            tokens = slice(t * P, (t + 1) * P)
+            g_tile = g_codes[c][:, tokens].bitcast(E5M2_X4)
+            g_tile_scales = g_scales[c][:, tokens]
+            steps = psum_mx.tile([P, BANK], F32, name="steps")
+            nc.tensor.matmul_mx(
+                out=steps[:],
+                lhsT=g_tile,
+                lhsT_scale=g_tile_scales,
+                rhs=plus_codes[:, 0:BANK].bitcast(E4M3_X4),
+                rhs_scale=plus_scales[:, 0:BANK],
+                start=True,
+                stop=False,
+            )
+            nc.tensor.matmul_mx(
+                out=steps[:],
+                lhsT=g_tile,
+                lhsT_scale=g_tile_scales,
+                rhs=minus_codes[:].bitcast(E4M3_X4),
+                rhs_scale=minus_scales[:],
+                start=False,
+                stop=True,
+            )
+            rest = psum_mx.tile([P, BANK], F32, name="rest")
+            nc.tensor.matmul_mx(
+                out=rest[:],
+                lhsT=g_tile,
+                lhsT_scale=g_tile_scales,
+                rhs=plus_codes[:, BANK : 2 * BANK].bitcast(E4M3_X4),
+                rhs_scale=plus_scales[:, BANK : 2 * BANK],
+                start=True,
+                stop=True,
+            )
+            nc.vector.scalar_tensor_tensor(
+                out=prod[c][:, t, BASES, :],
+                in0=dist[c][:, t, BASES, :],
+                scalar=1.0,
+                in1=rest[:, 0:IN_F],
+                op0=ALU.min,
+                op1=ALU.mult,
+            )
+            nc.vector.scalar_tensor_tensor(
+                out=prod[c][:, t, 0:BASES, :].rearrange("p j i -> p (j i)"),
+                in0=dist[c][:, t, 0:BASES, :].rearrange("p j i -> p (j i)"),
+                scalar=1.0,
+                in1=steps[:],
+                op0=ALU.min,
+                op1=ALU.mult,
+            )
+            nc.vector.tensor_tensor(
+                out=last[c][:, t, :], in0=prod[c][:, t, BASES, :], in1=rest[:, IN_F : 2 * IN_F], op=ALU.add
+            )
+
+        def add_four(c):
+            two = work.tile([P, TILES, 2, IN_F], F32, name="two")
+            nc.gpsimd.tensor_tensor(
+                out=two[:], in0=prod[c][:, :, 0:2, :], in1=prod[c][:, :, 2:4, :], op=ALU.add
+            )
+            four[c] = work.tile([P, TILES, IN_F], F32, name="four")
+            nc.gpsimd.tensor_tensor(out=four[c][:], in0=two[:, :, 0, :], in1=two[:, :, 1, :], op=ALU.add)
+
+        def finish(c):
+            out_sb = stores.tile([P, TILES, IN_F], F32, name="out_sb")
+            nc.vector.tensor_tensor(out=out_sb[:], in0=four[c][:], in1=last[c][:], op=ALU.add)
             nc.sync.dma_start(out=out_rows[c], in_=out_sb[:].rearrange("p t i -> p (t i)"))
+
+        for c in range(LOOKAHEAD):
+            load(c)
+        for i in range(-1, N_CHUNKS + 1):
+            if i + 1 + LOOKAHEAD < N_CHUNKS:
+                load(i + 1 + LOOKAHEAD)
+            if i + 1 < N_CHUNKS:
+                g_bf_next = transpose_and_measure(i + 1)
+            if 0 <= i < N_CHUNKS:
+                prod[i] = work.tile([P, TILES, HATS, IN_F], F32, name="prod")
+                last[i] = work.tile([P, TILES, IN_F], F32, name="last")
+                multiply(i, 0)
+                multiply(i, 1)
+            if i + 1 < N_CHUNKS:
+                quantise(i + 1, g_bf_next)
+            if 0 <= i < N_CHUNKS:
+                multiply(i, 2)
+                multiply(i, 3)
+            if 0 <= i - 1:
+                finish(i - 1)
+            if 0 <= i < N_CHUNKS:
+                add_four(i)

@@ -40,7 +40,7 @@ def tile_kanlayer_t_kernel(tc, x, base_weight, spline_weight, grid, grad_out, ou
     with (
         tc.tile_pool(name="keep", bufs=1) as keep,
         tc.tile_pool(name="loads", bufs=LOOKAHEAD + 1) as loads,
-        tc.tile_pool(name="work", bufs=2) as work,
+        tc.tile_pool(name="work", bufs=3) as work,
         tc.tile_pool(name="stores", bufs=3) as stores,
         tc.psum_pool(name="psum_t", bufs=2) as psum_t,
         tc.psum_pool(name="psum_mx", bufs=3) as psum_mx,
@@ -203,7 +203,7 @@ def tile_kanlayer_t_kernel(tc, x, base_weight, spline_weight, grid, grad_out, ou
 
         for c in range(LOOKAHEAD):
             load(c)
-        for i in range(-1, N_CHUNKS + 1):
+        for i in range(-1, N_CHUNKS + 2):
             if i + 1 + LOOKAHEAD < N_CHUNKS:
                 load(i + 1 + LOOKAHEAD)
             if i + 1 < N_CHUNKS:
@@ -218,7 +218,7 @@ def tile_kanlayer_t_kernel(tc, x, base_weight, spline_weight, grid, grad_out, ou
             if 0 <= i < N_CHUNKS:
                 multiply(i, 2)
                 multiply(i, 3)
-            if 0 <= i - 1:
-                finish(i - 1)
+            if 0 <= i - 2:
+                finish(i - 2)
             if 0 <= i < N_CHUNKS:
                 add_four(i)

@@ -123,7 +123,7 @@ def tile_kanlayer_t_kernel(tc, x, base_weight, spline_weight, grid, grad_out, ou
                     out=dist[c][:, :, j, :],
                     in_=x_sb[c][:],
                     func=ACT.Abs,
-                    bias=minus_centre[:, j : j + 1],
+                    bias=float(2 - j),
                     scale=1.0,
                 )
             return g_bf

@@ -40,7 +40,7 @@ def tile_kanlayer_t_kernel(tc, x, base_weight, spline_weight, grid, grad_out, ou
     with (
         tc.tile_pool(name="keep", bufs=1) as keep,
         tc.tile_pool(name="loads", bufs=LOOKAHEAD + 1) as loads,
-        tc.tile_pool(name="work", bufs=3) as work,
+        tc.tile_pool(name="work", bufs=2) as work,
         tc.tile_pool(name="stores", bufs=3) as stores,
         tc.psum_pool(name="psum_t", bufs=2) as psum_t,
         tc.psum_pool(name="psum_mx", bufs=3) as psum_mx,
@@ -93,7 +93,7 @@ def tile_kanlayer_t_kernel(tc, x, base_weight, spline_weight, grid, grad_out, ou
         out_rows = out.rearrange("(c p t) i -> c p (t i)", p=P, t=TILES)
 
 
-        g_sb, x_sb, g_codes, g_scales, dist, prod, last, four = {}, {}, {}, {}, {}, {}, {}, {}
+        g_sb, x_sb, g_codes, g_scales, dist, prod, last, two, four = {}, {}, {}, {}, {}, {}, {}, {}, {}
 
         def load(c):
             g_sb[c] = loads.tile([P, TILES * OUT_F], BF16, name="g_sb")
@@ -123,7 +123,7 @@ def tile_kanlayer_t_kernel(tc, x, base_weight, spline_weight, grid, grad_out, ou
                     out=dist[c][:, :, j, :],
                     in_=x_sb[c][:],
                     func=ACT.Abs,
-                    bias=float(2 - j),
+                    bias=minus_centre[:, j : j + 1],
                     scale=1.0,
                 )
             return g_bf
@@ -188,13 +188,17 @@ def tile_kanlayer_t_kernel(tc, x, base_weight, spline_weight, grid, grad_out, ou
                 out=last[c][:, t, :], in0=prod[c][:, t, BASES, :], in1=rest[:, IN_F : 2 * IN_F], op=ALU.add
             )
 
-        def add_four(c):
-            two = work.tile([P, TILES, 2, IN_F], F32, name="two")
+        def add_pairs(c):
+            two[c] = work.tile([P, TILES, 2, IN_F], F32, name="two")
             nc.gpsimd.tensor_tensor(
-                out=two[:], in0=prod[c][:, :, 0:2, :], in1=prod[c][:, :, 2:4, :], op=ALU.add
+                out=two[c][:], in0=prod[c][:, :, 0:2, :], in1=prod[c][:, :, 2:4, :], op=ALU.add
             )
+
+        def add_four(c):
             four[c] = work.tile([P, TILES, IN_F], F32, name="four")
-            nc.gpsimd.tensor_tensor(out=four[c][:], in0=two[:, :, 0, :], in1=two[:, :, 1, :], op=ALU.add)
+            nc.vector.tensor_tensor(
+                out=four[c][:], in0=two[c][:, :, 0, :], in1=two[c][:, :, 1, :], op=ALU.add
+            )
 
         def finish(c):
             out_sb = stores.tile([P, TILES, IN_F], F32, name="out_sb")
@@ -203,7 +207,7 @@ def tile_kanlayer_t_kernel(tc, x, base_weight, spline_weight, grid, grad_out, ou
 
         for c in range(LOOKAHEAD):
             load(c)
-        for i in range(-1, N_CHUNKS + 2):
+        for i in range(-1, N_CHUNKS + 1):
             if i + 1 + LOOKAHEAD < N_CHUNKS:
                 load(i + 1 + LOOKAHEAD)
             if i + 1 < N_CHUNKS:
@@ -213,12 +217,13 @@ def tile_kanlayer_t_kernel(tc, x, base_weight, spline_weight, grid, grad_out, ou
                 last[i] = work.tile([P, TILES, IN_F], F32, name="last")
                 multiply(i, 0)
                 multiply(i, 1)
+                multiply(i, 2)
+            if 0 <= i - 1:
+                add_four(i - 1)
             if i + 1 < N_CHUNKS:
                 quantise(i + 1, g_bf_next)
+            if 0 <= i - 1:
+                finish(i - 1)
             if 0 <= i < N_CHUNKS:
-                multiply(i, 2)
                 multiply(i, 3)
-            if 0 <= i - 2:
-                finish(i - 2)
-            if 0 <= i < N_CHUNKS:
-                add_four(i)
+                add_pairs(i)

@@ -20,9 +20,12 @@ HATS = BASES + 1
 BANK = 512
 HALF = OUT_F // 2
 TILES = 4
+RUN_TILES = 4
+RUNS = TILES // RUN_TILES
 CHUNK = P * TILES
 N_CHUNKS = TOKENS // CHUNK
-LOOKAHEAD = 3
+AHEAD = 2
+LOOKAHEAD = 2
 
 FLOPS = 2 * TOKENS * OUT_F * (IN_F + IN_F * BASES)
 
@@ -35,13 +38,17 @@ def load_weight_rows(nc, raw, weight):
         )
 
 
+def live(c):
+    return 0 <= c < N_CHUNKS
+
+
 def tile_kanlayer_t_kernel(tc, x, base_weight, spline_weight, grid, grad_out, out):
     nc = tc.nc
     with (
         tc.tile_pool(name="keep", bufs=1) as keep,
         tc.tile_pool(name="loads", bufs=LOOKAHEAD + 1) as loads,
+        tc.tile_pool(name="ready", bufs=AHEAD + 1) as ready,
         tc.tile_pool(name="work", bufs=2) as work,
-        tc.tile_pool(name="stores", bufs=3) as stores,
         tc.psum_pool(name="psum_t", bufs=2) as psum_t,
         tc.psum_pool(name="psum_mx", bufs=3) as psum_mx,
         tc.manual_schedule(),
@@ -93,7 +100,7 @@ def tile_kanlayer_t_kernel(tc, x, base_weight, spline_weight, grid, grad_out, ou
         out_rows = out.rearrange("(c p t) i -> c p (t i)", p=P, t=TILES)
 
 
-        g_sb, x_sb, g_codes, g_scales, dist, prod, last, two, four = {}, {}, {}, {}, {}, {}, {}, {}, {}
+        g_sb, x_sb, g_bf, g_codes, g_scales, dist, prod, last, four = {}, {}, {}, {}, {}, {}, {}, {}, {}
 
         def load(c):
             g_sb[c] = loads.tile([P, TILES * OUT_F], BF16, name="g_sb")
@@ -101,23 +108,26 @@ def tile_kanlayer_t_kernel(tc, x, base_weight, spline_weight, grid, grad_out, ou
             x_sb[c] = loads.tile([P, TILES, IN_F], BF16, name="x_sb")
             nc.sync.dma_start(out=x_sb[c][:].rearrange("p t i -> p (t i)"), in_=x_rows[c])
 
-        def transpose_and_measure(c):
+        def transpose(c, run):
+            if run == 0:
+                g_bf[c] = work.tile([P, TILES * OUT_F], BF16, align_bytes=64, name="g_bf")
             g_words = g_sb[c][:].bitcast(F32)
-            g_bf = work.tile([P, TILES * OUT_F], BF16, align_bytes=64, name="g_bf")
-            g_pairs = g_bf[:].bitcast(F32).rearrange("p (t r u) -> p t r u", r=P, u=2)
-            for pair in range(TILES // 2):
+            g_pairs = g_bf[c][:].bitcast(F32).rearrange("p (t r u) -> p t r u", r=P, u=2)
+            for t in range(run * RUN_TILES, (run + 1) * RUN_TILES, 2):
                 g_t = psum_t.tile([P, 4, P], F32, name="g_t")
                 for a in range(2):
                     for u in range(2):
-                        first = ((2 * pair + a) * 2 + u) * P
+                        first = ((t + a) * 2 + u) * P
                         nc.tensor.transpose(
                             g_t[:, 2 * a + u, :], g_words[:, first : first + P], ident[:]
                         )
                 nc.scalar.copy(
-                    out=g_pairs[:, 2 * pair : 2 * pair + 2, :, :],
+                    out=g_pairs[:, t : t + 2, :, :],
                     in_=g_t[:].rearrange("p (a u) r -> p a r u", u=2),
                 )
-            dist[c] = work.tile([P, TILES, HATS, IN_F], F32, name="dist")
+
+        def measure(c):
+            dist[c] = ready.tile([P, TILES, HATS, IN_F], F32, name="dist")
             for j in range(HATS):
                 nc.scalar.activation(
                     out=dist[c][:, :, j, :],
@@ -126,13 +136,12 @@ def tile_kanlayer_t_kernel(tc, x, base_weight, spline_weight, grid, grad_out, ou
                     bias=minus_centre[:, j : j + 1],
                     scale=1.0,
                 )
-            return g_bf
 
-        def quantise(c, g_bf):
-            g_codes[c] = work.tile([P, TILES * P], U32, align_bytes=64, name="g_codes")
-            g_scales[c] = work.tile([P, TILES * P], U8, align_bytes=64, name="g_scales")
+        def quantise(c):
+            g_codes[c] = ready.tile([P, TILES * P], U32, align_bytes=64, name="g_codes")
+            g_scales[c] = ready.tile([P, TILES * P], U8, align_bytes=64, name="g_scales")
             nc.vector.quantize_mx(
-                out=g_codes[c][:].bitcast(E5M2_X4), scales=g_scales[c][:], in_=g_bf[:]
+                out=g_codes[c][:].bitcast(E5M2_X4), scales=g_scales[c][:], in_=g_bf[c][:]
             )
 
         def multiply(c, t):
@@ -188,42 +197,38 @@ def tile_kanlayer_t_kernel(tc, x, base_weight, spline_weight, grid, grad_out, ou
                 out=last[c][:, t, :], in0=prod[c][:, t, BASES, :], in1=rest[:, IN_F : 2 * IN_F], op=ALU.add
             )
 
-        def add_pairs(c):
-            two[c] = work.tile([P, TILES, 2, IN_F], F32, name="two")
-            nc.gpsimd.tensor_tensor(
-                out=two[c][:], in0=prod[c][:, :, 0:2, :], in1=prod[c][:, :, 2:4, :], op=ALU.add
-            )
-
         def add_four(c):
-            four[c] = work.tile([P, TILES, IN_F], F32, name="four")
-            nc.vector.tensor_tensor(
-                out=four[c][:], in0=two[c][:, :, 0, :], in1=two[c][:, :, 1, :], op=ALU.add
+            two = work.tile([P, TILES, 2, IN_F], F32, name="two")
+            nc.gpsimd.tensor_tensor(
+                out=two[:], in0=prod[c][:, :, 0:2, :], in1=prod[c][:, :, 2:4, :], op=ALU.add
             )
+            four[c] = ready.tile([P, TILES, IN_F], F32, name="four")
+            nc.gpsimd.tensor_tensor(out=four[c][:], in0=two[:, :, 0, :], in1=two[:, :, 1, :], op=ALU.add)
 
         def finish(c):
-            out_sb = stores.tile([P, TILES, IN_F], F32, name="out_sb")
+            out_sb = work.tile([P, TILES, IN_F], F32, name="out_sb")
             nc.vector.tensor_tensor(out=out_sb[:], in0=four[c][:], in1=last[c][:], op=ALU.add)
             nc.sync.dma_start(out=out_rows[c], in_=out_sb[:].rearrange("p t i -> p (t i)"))
 
         for c in range(LOOKAHEAD):
             load(c)
-        for i in range(-1, N_CHUNKS + 1):
-            if i + 1 + LOOKAHEAD < N_CHUNKS:
-                load(i + 1 + LOOKAHEAD)
-            if i + 1 < N_CHUNKS:
-                g_bf_next = transpose_and_measure(i + 1)
-            if 0 <= i < N_CHUNKS:
+        for i in range(-AHEAD, N_CHUNKS + 2):
+            if live(i + AHEAD + LOOKAHEAD):
+                load(i + AHEAD + LOOKAHEAD)
+            if live(i):
                 prod[i] = work.tile([P, TILES, HATS, IN_F], F32, name="prod")
-                last[i] = work.tile([P, TILES, IN_F], F32, name="last")
-                multiply(i, 0)
-                multiply(i, 1)
-                multiply(i, 2)
-            if 0 <= i - 1:
-                add_four(i - 1)
-            if i + 1 < N_CHUNKS:
-                quantise(i + 1, g_bf_next)
-            if 0 <= i - 1:
-                finish(i - 1)
-            if 0 <= i < N_CHUNKS:
-                multiply(i, 3)
-                add_pairs(i)
+                last[i] = ready.tile([P, TILES, IN_F], F32, name="last")
+            for run in range(RUNS):
+                if live(i + AHEAD):
+                    transpose(i + AHEAD, run)
+                    if run == 0:
+                        measure(i + AHEAD)
+                if live(i):
+                    for t in range(run * RUN_TILES, (run + 1) * RUN_TILES):
+                        multiply(i, t)
+            if live(i - 2):
+                finish(i - 2)
+            if live(i + AHEAD):
+                quantise(i + AHEAD)
+            if live(i):
+                add_four(i)

@@ -17,14 +17,13 @@ OUT_F = 512
 IN_F = 128
 BASES = 4
 HATS = BASES + 1
-BANK = 512
 HALF = OUT_F // 2
 TILES = 4
-RUN_TILES = 4
-RUNS = TILES // RUN_TILES
 CHUNK = P * TILES
 N_CHUNKS = TOKENS // CHUNK
-AHEAD = 2
+G_AHEAD = 2
+X_AHEAD = 1
+BACK = 2
 LOOKAHEAD = 2
 
 FLOPS = 2 * TOKENS * OUT_F * (IN_F + IN_F * BASES)
@@ -47,10 +46,12 @@ def tile_kanlayer_t_kernel(tc, x, base_weight, spline_weight, grid, grad_out, ou
     with (
         tc.tile_pool(name="keep", bufs=1) as keep,
         tc.tile_pool(name="loads", bufs=LOOKAHEAD + 1) as loads,
-        tc.tile_pool(name="ready", bufs=AHEAD + 1) as ready,
+        tc.tile_pool(name="loads_x", bufs=LOOKAHEAD + 2) as loads_x,
         tc.tile_pool(name="work", bufs=2) as work,
-        tc.psum_pool(name="psum_t", bufs=2) as psum_t,
-        tc.psum_pool(name="psum_mx", bufs=3) as psum_mx,
+        tc.psum_pool(name="psum_g", bufs=2) as psum_g,
+        tc.psum_pool(name="psum_x", bufs=1) as psum_x,
+        tc.psum_pool(name="psum_o", bufs=1) as psum_o,
+        tc.psum_pool(name="psum_mx", bufs=4) as psum_mx,
         tc.manual_schedule(),
     ):
         raw_sw = keep.tile([P, PACK, BASES * IN_F], BF16)
@@ -59,35 +60,54 @@ def tile_kanlayer_t_kernel(tc, x, base_weight, spline_weight, grid, grad_out, ou
         load_weight_rows(nc, raw_bw, base_weight)
         by_basis = raw_sw[:].rearrange("p k (i l) -> p l i k", l=BASES)
 
-        plus_bf = keep.tile([P, 2 * BASES, IN_F, PACK], BF16, align_bytes=64)
-        nc.vector.memset(plus_bf[:, 0, :, :], 0.0)
-        nc.vector.memset(plus_bf[:, BASES + 2 :, :, :], 0.0)
-        nc.vector.tensor_copy(out=plus_bf[:, 1 : BASES + 1, :, :], in_=by_basis)
-        nc.vector.tensor_copy(
-            out=plus_bf[:, BASES + 1, :, :], in_=raw_bw[:].rearrange("p k i -> p i k")
-        )
+        plus_bf = keep.tile([P, BASES, IN_F, PACK], BF16, align_bytes=64)
+        nc.vector.tensor_copy(out=plus_bf[:], in_=by_basis)
         minus_bf = keep.tile([P, BASES, IN_F, PACK], BF16, align_bytes=64)
         nc.vector.tensor_scalar(
             out=minus_bf[:], in0=by_basis, scalar1=-1.0, scalar2=None, op0=ALU.mult
         )
+        bw_bf = keep.tile([P, IN_F, PACK], BF16, align_bytes=64)
+        nc.vector.tensor_copy(out=bw_bf[:], in_=raw_bw[:].rearrange("p k i -> p i k"))
 
-        plus_codes = keep.tile([P, 2 * BANK], U32, align_bytes=64)
-        plus_scales = keep.tile([P, 2 * BANK], U8, align_bytes=64)
+        plus_codes = keep.tile([P, BASES * IN_F], U32, align_bytes=64)
+        plus_scales = keep.tile([P, BASES * IN_F], U8, align_bytes=64)
         nc.vector.quantize_mx(
             out=plus_codes[:].bitcast(E4M3_X4),
             scales=plus_scales[:],
             in_=plus_bf[:].rearrange("p a i k -> p (a i k)"),
         )
-        minus_codes = keep.tile([P, BANK], U32, align_bytes=64)
-        minus_scales = keep.tile([P, BANK], U8, align_bytes=64)
+        minus_codes = keep.tile([P, BASES * IN_F], U32, align_bytes=64)
+        minus_scales = keep.tile([P, BASES * IN_F], U8, align_bytes=64)
         nc.vector.quantize_mx(
             out=minus_codes[:].bitcast(E4M3_X4),
             scales=minus_scales[:],
             in_=minus_bf[:].rearrange("p a i k -> p (a i k)"),
         )
+        bw_codes = keep.tile([P, IN_F], U32, align_bytes=64)
+        bw_scales = keep.tile([P, IN_F], U8, align_bytes=64)
+        nc.vector.quantize_mx(
+            out=bw_codes[:].bitcast(E4M3_X4),
+            scales=bw_scales[:],
+            in_=bw_bf[:].rearrange("p i k -> p (i k)"),
+        )
+
+        def plane(codes, scales, a):
+            cols = slice(a * IN_F, (a + 1) * IN_F)
+            return codes[:, cols].bitcast(E4M3_X4), scales[:, cols]
+
+        passes_of = {}
+        for j in range(HATS):
+            passes_of[j] = []
+            if j > 0:
+                passes_of[j].append(plane(plus_codes, plus_scales, j - 1))
+            if j < BASES:
+                passes_of[j].append(plane(minus_codes, minus_scales, j))
+        passes_of["base"] = [plane(bw_codes, bw_scales, 0)]
 
         ident = keep.tile([P, P], F32)
         make_identity(nc, ident[:])
+        ident_bf = keep.tile([P, P], BF16)
+        make_identity(nc, ident_bf[:])
         grid_bf = keep.tile([P, HATS + 2], BF16)
         nc.sync.dma_start(out=grid_bf[:], in_=grid.partition_broadcast(P))
         minus_centre = keep.tile([P, HATS], F32)
@@ -99,22 +119,20 @@ def tile_kanlayer_t_kernel(tc, x, base_weight, spline_weight, grid, grad_out, ou
         x_rows = x.rearrange("(c p t) i -> c p (t i)", p=P, t=TILES)
         out_rows = out.rearrange("(c p t) i -> c p (t i)", p=P, t=TILES)
 
-
-        g_sb, x_sb, g_bf, g_codes, g_scales, dist, prod, last, four = {}, {}, {}, {}, {}, {}, {}, {}, {}
+        g_sb, x_sb, g_bf, g_codes, g_scales, dist, prod, pair, last = {}, {}, {}, {}, {}, {}, {}, {}, {}
 
         def load(c):
             g_sb[c] = loads.tile([P, TILES * OUT_F], BF16, name="g_sb")
             nc.sync.dma_start(out=g_sb[c][:], in_=g_rows[c])
-            x_sb[c] = loads.tile([P, TILES, IN_F], BF16, name="x_sb")
+            x_sb[c] = loads_x.tile([P, TILES, IN_F], BF16, name="x_sb")
             nc.sync.dma_start(out=x_sb[c][:].rearrange("p t i -> p (t i)"), in_=x_rows[c])
 
-        def transpose(c, run):
-            if run == 0:
-                g_bf[c] = work.tile([P, TILES * OUT_F], BF16, align_bytes=64, name="g_bf")
+        def turn_g(c):
+            g_bf[c] = work.tile([P, TILES * OUT_F], BF16, align_bytes=64, name="g_bf")
             g_words = g_sb[c][:].bitcast(F32)
             g_pairs = g_bf[c][:].bitcast(F32).rearrange("p (t r u) -> p t r u", r=P, u=2)
-            for t in range(run * RUN_TILES, (run + 1) * RUN_TILES, 2):
-                g_t = psum_t.tile([P, 4, P], F32, name="g_t")
+            for t in range(0, TILES, 2):
+                g_t = psum_g.tile([P, 4, P], F32, name="g_t")
                 for a in range(2):
                     for u in range(2):
                         first = ((t + a) * 2 + u) * P
@@ -126,109 +144,101 @@ def tile_kanlayer_t_kernel(tc, x, base_weight, spline_weight, grid, grad_out, ou
                     in_=g_t[:].rearrange("p (a u) r -> p a r u", u=2),
                 )
 
-        def measure(c):
-            dist[c] = ready.tile([P, TILES, HATS, IN_F], F32, name="dist")
+        def turn_x(c):
+            x_t = psum_x.tile([P, CHUNK], BF16, name="x_t")
+            for t in range(TILES):
+                nc.tensor.transpose(x_t[:, t * P : (t + 1) * P], x_sb[c][:, t, :], ident_bf[:])
+            dist[c] = work.tile([P, HATS, CHUNK], F32, name="dist")
             for j in range(HATS):
                 nc.scalar.activation(
-                    out=dist[c][:, :, j, :],
-                    in_=x_sb[c][:],
+                    out=dist[c][:, j, :],
+                    in_=x_t[:],
                     func=ACT.Abs,
                     bias=minus_centre[:, j : j + 1],
                     scale=1.0,
                 )
 
         def quantise(c):
-            g_codes[c] = ready.tile([P, TILES * P], U32, align_bytes=64, name="g_codes")
-            g_scales[c] = ready.tile([P, TILES * P], U8, align_bytes=64, name="g_scales")
+            g_codes[c] = work.tile([P, CHUNK], U32, align_bytes=64, name="g_codes")
+            g_scales[c] = work.tile([P, CHUNK], U8, align_bytes=64, name="g_scales")
             nc.vector.quantize_mx(
                 out=g_codes[c][:].bitcast(E5M2_X4), scales=g_scales[c][:], in_=g_bf[c][:]
             )
 
-        def multiply(c, t):
-            tokens = slice(t * P, (t + 1) * P)
-            g_tile = g_codes[c][:, tokens].bitcast(E5M2_X4)
-            g_tile_scales = g_scales[c][:, tokens]
-            steps = psum_mx.tile([P, BANK], F32, name="steps")
-            nc.tensor.matmul_mx(
-                out=steps[:],
-                lhsT=g_tile,
-                lhsT_scale=g_tile_scales,
-                rhs=plus_codes[:, 0:BANK].bitcast(E4M3_X4),
-                rhs_scale=plus_scales[:, 0:BANK],
-                start=True,
-                stop=False,
-            )
-            nc.tensor.matmul_mx(
-                out=steps[:],
-                lhsT=g_tile,
-                lhsT_scale=g_tile_scales,
-                rhs=minus_codes[:].bitcast(E4M3_X4),
-                rhs_scale=minus_scales[:],
-                start=False,
-                stop=True,
-            )
-            rest = psum_mx.tile([P, BANK], F32, name="rest")
-            nc.tensor.matmul_mx(
-                out=rest[:],
-                lhsT=g_tile,
-                lhsT_scale=g_tile_scales,
-                rhs=plus_codes[:, BANK : 2 * BANK].bitcast(E4M3_X4),
-                rhs_scale=plus_scales[:, BANK : 2 * BANK],
-                start=True,
-                stop=True,
-            )
+        def matmuls(c, which):
+            acc = psum_mx.tile([P, CHUNK], F32, name="acc")
+            passes = passes_of[which]
+            for n, (codes, scales) in enumerate(passes):
+                nc.tensor.matmul_mx(
+                    out=acc[:],
+                    lhsT=codes,
+                    lhsT_scale=scales,
+                    rhs=g_codes[c][:].bitcast(E5M2_X4),
+                    rhs_scale=g_scales[c][:],
+                    start=(n == 0),
+                    stop=(n == len(passes) - 1),
+                )
+            return acc
+
+        def product(c, j):
+            acc = matmuls(c, j)
             nc.vector.scalar_tensor_tensor(
-                out=prod[c][:, t, BASES, :],
-                in0=dist[c][:, t, BASES, :],
+                out=prod[c][:, j, :],
+                in0=dist[c][:, j, :],
                 scalar=1.0,
-                in1=rest[:, 0:IN_F],
+                in1=acc[:],
                 op0=ALU.min,
                 op1=ALU.mult,
             )
-            nc.vector.scalar_tensor_tensor(
-                out=prod[c][:, t, 0:BASES, :].rearrange("p j i -> p (j i)"),
-                in0=dist[c][:, t, 0:BASES, :].rearrange("p j i -> p (j i)"),
-                scalar=1.0,
-                in1=steps[:],
-                op0=ALU.min,
-                op1=ALU.mult,
-            )
-            nc.vector.tensor_tensor(
-                out=last[c][:, t, :], in0=prod[c][:, t, BASES, :], in1=rest[:, IN_F : 2 * IN_F], op=ALU.add
-            )
 
-        def add_four(c):
-            two = work.tile([P, TILES, 2, IN_F], F32, name="two")
-            nc.gpsimd.tensor_tensor(
-                out=two[:], in0=prod[c][:, :, 0:2, :], in1=prod[c][:, :, 2:4, :], op=ALU.add
-            )
-            four[c] = ready.tile([P, TILES, IN_F], F32, name="four")
-            nc.gpsimd.tensor_tensor(out=four[c][:], in0=two[:, :, 0, :], in1=two[:, :, 1, :], op=ALU.add)
+        def multiply(c):
+            prod[c] = work.tile([P, HATS, CHUNK], F32, name="prod")
+            pair[c] = work.tile([P, 2, CHUNK], F32, name="pair")
+            last[c] = work.tile([P, CHUNK], F32, name="last")
+            product(c, BASES)
+            if live(c + X_AHEAD):
+                quantise(c + X_AHEAD)
+            for half in range(2):
+                product(c, 2 * half)
+                product(c, 2 * half + 1)
+                nc.gpsimd.tensor_tensor(
+                    out=pair[c][:, half, :],
+                    in0=prod[c][:, 2 * half, :],
+                    in1=prod[c][:, 2 * half + 1, :],
+                    op=ALU.add,
+                )
+            acc = matmuls(c, "base")
+            nc.vector.tensor_tensor(out=last[c][:], in0=prod[c][:, BASES, :], in1=acc[:], op=ALU.add)
 
-        def finish(c):
+        def turn_back(c):
+            out_ps = psum_o.tile([P, TILES, IN_F], F32, name="out_ps")
+            terms = [pair[c][:, 0, :], pair[c][:, 1, :], last[c][:]]
+            for t in range(TILES):
+                for n, term in enumerate(terms):
+                    nc.tensor.matmul(
+                        out_ps[:, t, :],
+                        lhsT=term[:, t * P : (t + 1) * P],
+                        rhs=ident[:],
+                        start=(n == 0),
+                        stop=(n == len(terms) - 1),
+                        is_transpose=True,
+                    )
             out_sb = work.tile([P, TILES, IN_F], F32, name="out_sb")
-            nc.vector.tensor_tensor(out=out_sb[:], in0=four[c][:], in1=last[c][:], op=ALU.add)
+            nc.scalar.copy(out=out_sb[:], in_=out_ps[:])
             nc.sync.dma_start(out=out_rows[c], in_=out_sb[:].rearrange("p t i -> p (t i)"))
 
         for c in range(LOOKAHEAD):
             load(c)
-        for i in range(-AHEAD, N_CHUNKS + 2):
-            if live(i + AHEAD + LOOKAHEAD):
-                load(i + AHEAD + LOOKAHEAD)
+        for i in range(-G_AHEAD, N_CHUNKS + BACK):
+            if live(i + G_AHEAD + LOOKAHEAD):
+                load(i + G_AHEAD + LOOKAHEAD)
+            if live(i - BACK):
+                turn_back(i - BACK)
+            if live(i + G_AHEAD):
+                turn_g(i + G_AHEAD)
+            if live(i + X_AHEAD):
+                turn_x(i + X_AHEAD)
             if live(i):
-                prod[i] = work.tile([P, TILES, HATS, IN_F], F32, name="prod")
-                last[i] = ready.tile([P, TILES, IN_F], F32, name="last")
-            for run in range(RUNS):
-                if live(i + AHEAD):
-                    transpose(i + AHEAD, run)
-                    if run == 0:
-                        measure(i + AHEAD)
-                if live(i):
-                    for t in range(run * RUN_TILES, (run + 1) * RUN_TILES):
-                        multiply(i, t)
-            if live(i - 2):
-                finish(i - 2)
-            if live(i + AHEAD):
-                quantise(i + AHEAD)
-            if live(i):
-                add_four(i)
+                multiply(i)
+            elif live(i + X_AHEAD):
+                quantise(i + X_AHEAD)

@@ -196,17 +196,15 @@ def tile_kanlayer_t_kernel(tc, x, base_weight, spline_weight, grid, grad_out, ou
             pair[c] = work.tile([P, 2, CHUNK], F32, name="pair")
             last[c] = work.tile([P, CHUNK], F32, name="last")
             product(c, BASES)
+            product(c, 0)
+            product(c, 1)
+            product(c, 2)
             if live(c + X_AHEAD):
                 quantise(c + X_AHEAD)
-            for half in range(2):
-                product(c, 2 * half)
-                product(c, 2 * half + 1)
-                nc.gpsimd.tensor_tensor(
-                    out=pair[c][:, half, :],
-                    in0=prod[c][:, 2 * half, :],
-                    in1=prod[c][:, 2 * half + 1, :],
-                    op=ALU.add,
-                )
+            product(c, 3)
+            nc.gpsimd.tensor_tensor(
+                out=pair[c][:], in0=prod[c][:, 0:2, :], in1=prod[c][:, 2:4, :], op=ALU.add
+            )
             acc = matmuls(c, "base")
             nc.vector.tensor_tensor(out=last[c][:], in0=prod[c][:, BASES, :], in1=acc[:], op=ALU.add)
 

@@ -21,10 +21,12 @@ HALF = OUT_F // 2
 TILES = 4
 CHUNK = P * TILES
 N_CHUNKS = TOKENS // CHUNK
+LAST_CHUNK = N_CHUNKS - 1
 G_AHEAD = 2
 X_AHEAD = 1
-BACK = 2
+BACK = 3
 LOOKAHEAD = 2
+FOLDED = 2
 
 FLOPS = 2 * TOKENS * OUT_F * (IN_F + IN_F * BASES)
 
@@ -48,6 +50,7 @@ def tile_kanlayer_t_kernel(tc, x, base_weight, spline_weight, grid, grad_out, ou
         tc.tile_pool(name="loads", bufs=LOOKAHEAD + 1) as loads,
         tc.tile_pool(name="loads_x", bufs=LOOKAHEAD + 2) as loads_x,
         tc.tile_pool(name="work", bufs=2) as work,
+        tc.tile_pool(name="terms", bufs=BACK) as terms_pool,
         tc.psum_pool(name="psum_g", bufs=2) as psum_g,
         tc.psum_pool(name="psum_x", bufs=1) as psum_x,
         tc.psum_pool(name="psum_o", bufs=1) as psum_o,
@@ -62,12 +65,12 @@ def tile_kanlayer_t_kernel(tc, x, base_weight, spline_weight, grid, grad_out, ou
 
         plus_bf = keep.tile([P, BASES, IN_F, PACK], BF16, align_bytes=64)
         nc.vector.tensor_copy(out=plus_bf[:], in_=by_basis)
-        minus_bf = keep.tile([P, BASES, IN_F, PACK], BF16, align_bytes=64)
-        nc.vector.tensor_scalar(
-            out=minus_bf[:], in0=by_basis, scalar1=-1.0, scalar2=None, op0=ALU.mult
-        )
         bw_bf = keep.tile([P, IN_F, PACK], BF16, align_bytes=64)
         nc.vector.tensor_copy(out=bw_bf[:], in_=raw_bw[:].rearrange("p k i -> p i k"))
+        minus_bf = keep.tile([P, BASES, IN_F, PACK], BF16, align_bytes=64)
+        nc.vector.tensor_scalar(
+            out=minus_bf[:], in0=plus_bf[:], scalar1=-1.0, scalar2=None, op0=ALU.mult
+        )
 
         plus_codes = keep.tile([P, BASES * IN_F], U32, align_bytes=64)
         plus_scales = keep.tile([P, BASES * IN_F], U8, align_bytes=64)
@@ -109,7 +112,7 @@ def tile_kanlayer_t_kernel(tc, x, base_weight, spline_weight, grid, grad_out, ou
         ident_bf = keep.tile([P, P], BF16)
         make_identity(nc, ident_bf[:])
         grid_bf = keep.tile([P, HATS + 2], BF16)
-        nc.sync.dma_start(out=grid_bf[:], in_=grid.partition_broadcast(P))
+        nc.scalar.dma_start(out=grid_bf[:], in_=grid.partition_broadcast(P))
         minus_centre = keep.tile([P, HATS], F32)
         nc.vector.tensor_scalar(
             out=minus_centre[:], in0=grid_bf[:, 1 : HATS + 1], scalar1=-1.0, scalar2=None, op0=ALU.mult
@@ -119,7 +122,7 @@ def tile_kanlayer_t_kernel(tc, x, base_weight, spline_weight, grid, grad_out, ou
         x_rows = x.rearrange("(c p t) i -> c p (t i)", p=P, t=TILES)
         out_rows = out.rearrange("(c p t) i -> c p (t i)", p=P, t=TILES)
 
-        g_sb, x_sb, g_bf, g_codes, g_scales, dist, prod, pair, last = {}, {}, {}, {}, {}, {}, {}, {}, {}
+        g_sb, x_sb, g_bf, g_codes, g_scales, dist, prod, pair, last, four = {}, {}, {}, {}, {}, {}, {}, {}, {}, {}
 
         def load(c):
             g_sb[c] = loads.tile([P, TILES * OUT_F], BF16, name="g_sb")
@@ -191,27 +194,42 @@ def tile_kanlayer_t_kernel(tc, x, base_weight, spline_weight, grid, grad_out, ou
                 op1=ALU.mult,
             )
 
+        def fold(c):
+            four[c] = work.tile([P, FOLDED * P], F32, name="four")
+            nc.vector.tensor_tensor(
+                out=four[c][:], in0=pair[c][:, 0, 0 : FOLDED * P], in1=pair[c][:, 1, 0 : FOLDED * P], op=ALU.add
+            )
+
         def multiply(c):
             prod[c] = work.tile([P, HATS, CHUNK], F32, name="prod")
-            pair[c] = work.tile([P, 2, CHUNK], F32, name="pair")
-            last[c] = work.tile([P, CHUNK], F32, name="last")
+            if c != LAST_CHUNK:
+                pair[c] = terms_pool.tile([P, 2, CHUNK], F32, name="pair")
+            last[c] = terms_pool.tile([P, CHUNK], F32, name="last")
             product(c, BASES)
             product(c, 0)
             product(c, 1)
             product(c, 2)
+            if live(c - 1):
+                fold(c - 1)
             if live(c + X_AHEAD):
                 quantise(c + X_AHEAD)
             product(c, 3)
-            nc.gpsimd.tensor_tensor(
-                out=pair[c][:], in0=prod[c][:, 0:2, :], in1=prod[c][:, 2:4, :], op=ALU.add
-            )
+            if c != LAST_CHUNK:
+                nc.gpsimd.tensor_tensor(
+                    out=pair[c][:], in0=prod[c][:, 0:2, :], in1=prod[c][:, 2:4, :], op=ALU.add
+                )
             acc = matmuls(c, "base")
             nc.vector.tensor_tensor(out=last[c][:], in0=prod[c][:, BASES, :], in1=acc[:], op=ALU.add)
 
         def turn_back(c):
             out_ps = psum_o.tile([P, TILES, IN_F], F32, name="out_ps")
-            terms = [pair[c][:, 0, :], pair[c][:, 1, :], last[c][:]]
             for t in range(TILES):
+                if c == LAST_CHUNK:
+                    terms = [prod[c][:, j, :] for j in range(BASES)] + [last[c][:]]
+                elif t < FOLDED:
+                    terms = [four[c][:], last[c][:]]
+                else:
+                    terms = [pair[c][:, 0, :], pair[c][:, 1, :], last[c][:]]
                 for n, term in enumerate(terms):
                     nc.tensor.matmul(
                         out_ps[:, t, :],

@@ -50,6 +50,8 @@ def tile_kanlayer_t_kernel(tc, x, base_weight, spline_weight, grid, grad_out, ou
         tc.tile_pool(name="loads", bufs=LOOKAHEAD + 1) as loads,
         tc.tile_pool(name="loads_x", bufs=LOOKAHEAD + 2) as loads_x,
         tc.tile_pool(name="work", bufs=2) as work,
+        tc.tile_pool(name="work3", bufs=3) as work3,
+        tc.tile_pool(name="stores", bufs=N_CHUNKS) as stores,
         tc.tile_pool(name="terms", bufs=BACK) as terms_pool,
         tc.psum_pool(name="psum_g", bufs=2) as psum_g,
         tc.psum_pool(name="psum_x", bufs=1) as psum_x,
@@ -131,7 +133,7 @@ def tile_kanlayer_t_kernel(tc, x, base_weight, spline_weight, grid, grad_out, ou
             nc.sync.dma_start(out=x_sb[c][:].rearrange("p t i -> p (t i)"), in_=x_rows[c])
 
         def turn_g(c):
-            g_bf[c] = work.tile([P, TILES * OUT_F], BF16, align_bytes=64, name="g_bf")
+            g_bf[c] = work3.tile([P, TILES * OUT_F], BF16, align_bytes=64, name="g_bf")
             g_words = g_sb[c][:].bitcast(F32)
             g_pairs = g_bf[c][:].bitcast(F32).rearrange("p (t r u) -> p t r u", r=P, u=2)
             for t in range(0, TILES, 2):
@@ -151,7 +153,7 @@ def tile_kanlayer_t_kernel(tc, x, base_weight, spline_weight, grid, grad_out, ou
             x_t = psum_x.tile([P, CHUNK], BF16, name="x_t")
             for t in range(TILES):
                 nc.tensor.transpose(x_t[:, t * P : (t + 1) * P], x_sb[c][:, t, :], ident_bf[:])
-            dist[c] = work.tile([P, HATS, CHUNK], F32, name="dist")
+            dist[c] = work3.tile([P, HATS, CHUNK], F32, name="dist")
             for j in range(HATS):
                 nc.scalar.activation(
                     out=dist[c][:, j, :],
@@ -239,7 +241,7 @@ def tile_kanlayer_t_kernel(tc, x, base_weight, spline_weight, grid, grad_out, ou
                         stop=(n == len(terms) - 1),
                         is_transpose=True,
                     )
-            out_sb = work.tile([P, TILES, IN_F], F32, name="out_sb")
+            out_sb = stores.tile([P, TILES, IN_F], F32, name="out_sb")
             nc.scalar.copy(out=out_sb[:], in_=out_ps[:])
             nc.sync.dma_start(out=out_rows[c], in_=out_sb[:].rearrange("p t i -> p (t i)"))
 

@@ -28,6 +28,8 @@ BACK = 3
 LOOKAHEAD = 2
 FOLDED = 2
 
+NEGATIVE = (0, 2, 4)
+
 FLOPS = 2 * TOKENS * OUT_F * (IN_F + IN_F * BASES)
 
 
@@ -37,6 +39,10 @@ def load_weight_rows(nc, raw, weight):
             out=raw[:, 2 * u : 2 * u + 2, :],
             in_=weight[HALF * u : HALF * (u + 1), :].rearrange("(p e) c -> p e c", e=2),
         )
+
+
+def folded(c):
+    return 0 <= c <= LAST_CHUNK - BACK
 
 
 def live(c):
@@ -51,6 +57,7 @@ def tile_kanlayer_t_kernel(tc, x, base_weight, spline_weight, grid, grad_out, ou
         tc.tile_pool(name="loads_x", bufs=LOOKAHEAD + 2) as loads_x,
         tc.tile_pool(name="work", bufs=2) as work,
         tc.tile_pool(name="work3", bufs=3) as work3,
+        tc.tile_pool(name="shared", bufs=6) as shared,
         tc.tile_pool(name="stores", bufs=N_CHUNKS) as stores,
         tc.tile_pool(name="terms", bufs=BACK) as terms_pool,
         tc.psum_pool(name="psum_g", bufs=2) as psum_g,
@@ -65,49 +72,41 @@ def tile_kanlayer_t_kernel(tc, x, base_weight, spline_weight, grid, grad_out, ou
         load_weight_rows(nc, raw_bw, base_weight)
         by_basis = raw_sw[:].rearrange("p k (i l) -> p l i k", l=BASES)
 
-        plus_bf = keep.tile([P, BASES, IN_F, PACK], BF16, align_bytes=64)
-        nc.vector.tensor_copy(out=plus_bf[:], in_=by_basis)
-        bw_bf = keep.tile([P, IN_F, PACK], BF16, align_bytes=64)
-        nc.vector.tensor_copy(out=bw_bf[:], in_=raw_bw[:].rearrange("p k i -> p i k"))
-        minus_bf = keep.tile([P, BASES, IN_F, PACK], BF16, align_bytes=64)
+        signed_bf = keep.tile([P, BASES, IN_F, PACK], BF16, align_bytes=64)
+        nc.vector.tensor_copy(out=signed_bf[:, 0:BASES:2], in_=by_basis[:, 0:BASES:2])
         nc.vector.tensor_scalar(
-            out=minus_bf[:], in0=plus_bf[:], scalar1=-1.0, scalar2=None, op0=ALU.mult
+            out=signed_bf[:, 1:BASES:2],
+            in0=by_basis[:, 1:BASES:2],
+            scalar1=-1.0,
+            scalar2=None,
+            op0=ALU.mult,
         )
-
-        plus_codes = keep.tile([P, BASES * IN_F], U32, align_bytes=64)
-        plus_scales = keep.tile([P, BASES * IN_F], U8, align_bytes=64)
+        sw_codes = keep.tile([P, BASES * IN_F], U32, align_bytes=64)
+        sw_scales = keep.tile([P, BASES * IN_F], U8, align_bytes=64)
         nc.vector.quantize_mx(
-            out=plus_codes[:].bitcast(E4M3_X4),
-            scales=plus_scales[:],
-            in_=plus_bf[:].rearrange("p a i k -> p (a i k)"),
+            out=sw_codes[:].bitcast(E4M3_X4),
+            scales=sw_scales[:],
+            in_=signed_bf[:].rearrange("p a i k -> p (a i k)"),
         )
-        minus_codes = keep.tile([P, BASES * IN_F], U32, align_bytes=64)
-        minus_scales = keep.tile([P, BASES * IN_F], U8, align_bytes=64)
-        nc.vector.quantize_mx(
-            out=minus_codes[:].bitcast(E4M3_X4),
-            scales=minus_scales[:],
-            in_=minus_bf[:].rearrange("p a i k -> p (a i k)"),
-        )
+        bw_bf = keep.tile([P, IN_F, PACK], BF16, align_bytes=64)
         bw_codes = keep.tile([P, IN_F], U32, align_bytes=64)
         bw_scales = keep.tile([P, IN_F], U8, align_bytes=64)
-        nc.vector.quantize_mx(
-            out=bw_codes[:].bitcast(E4M3_X4),
-            scales=bw_scales[:],
-            in_=bw_bf[:].rearrange("p i k -> p (i k)"),
-        )
+
+        def prepare_base():
+            nc.vector.tensor_copy(out=bw_bf[:], in_=raw_bw[:].rearrange("p k i -> p i k"))
+            nc.vector.quantize_mx(
+                out=bw_codes[:].bitcast(E4M3_X4),
+                scales=bw_scales[:],
+                in_=bw_bf[:].rearrange("p i k -> p (i k)"),
+            )
 
         def plane(codes, scales, a):
             cols = slice(a * IN_F, (a + 1) * IN_F)
             return codes[:, cols].bitcast(E4M3_X4), scales[:, cols]
 
-        passes_of = {}
+        passes_of = {"base": [plane(bw_codes, bw_scales, 0)]}
         for j in range(HATS):
-            passes_of[j] = []
-            if j > 0:
-                passes_of[j].append(plane(plus_codes, plus_scales, j - 1))
-            if j < BASES:
-                passes_of[j].append(plane(minus_codes, minus_scales, j))
-        passes_of["base"] = [plane(bw_codes, bw_scales, 0)]
+            passes_of[j] = [plane(sw_codes, sw_scales, l) for l in (j - 1, j) if 0 <= l < BASES]
 
         ident = keep.tile([P, P], F32)
         make_identity(nc, ident[:])
@@ -116,7 +115,7 @@ def tile_kanlayer_t_kernel(tc, x, base_weight, spline_weight, grid, grad_out, ou
         grid_bf = keep.tile([P, HATS + 2], BF16)
         nc.scalar.dma_start(out=grid_bf[:], in_=grid.partition_broadcast(P))
         minus_centre = keep.tile([P, HATS], F32)
-        nc.vector.tensor_scalar(
+        nc.gpsimd.tensor_scalar(
             out=minus_centre[:], in0=grid_bf[:, 1 : HATS + 1], scalar1=-1.0, scalar2=None, op0=ALU.mult
         )
 
@@ -133,7 +132,7 @@ def tile_kanlayer_t_kernel(tc, x, base_weight, spline_weight, grid, grad_out, ou
             nc.sync.dma_start(out=x_sb[c][:].rearrange("p t i -> p (t i)"), in_=x_rows[c])
 
         def turn_g(c):
-            g_bf[c] = work3.tile([P, TILES * OUT_F], BF16, align_bytes=64, name="g_bf")
+            g_bf[c] = shared.tile([P, TILES * OUT_F], BF16, align_bytes=64, name="g_bf")
             g_words = g_sb[c][:].bitcast(F32)
             g_pairs = g_bf[c][:].bitcast(F32).rearrange("p (t r u) -> p t r u", r=P, u=2)
             for t in range(0, TILES, 2):
@@ -162,6 +161,11 @@ def tile_kanlayer_t_kernel(tc, x, base_weight, spline_weight, grid, grad_out, ou
                     bias=minus_centre[:, j : j + 1],
                     scale=1.0,
                 )
+            if c == LAST_CHUNK:
+                for j in NEGATIVE:
+                    nc.scalar.activation(
+                        out=dist[c][:, j, :], in_=dist[c][:, j, :], func=ACT.Relu, bias=1.0, scale=-1.0
+                    )
 
         def quantise(c):
             g_codes[c] = work.tile([P, CHUNK], U32, align_bytes=64, name="g_codes")
@@ -187,12 +191,13 @@ def tile_kanlayer_t_kernel(tc, x, base_weight, spline_weight, grid, grad_out, ou
 
         def product(c, j):
             acc = matmuls(c, j)
+            signed = c == LAST_CHUNK and j in NEGATIVE
             nc.vector.scalar_tensor_tensor(
                 out=prod[c][:, j, :],
                 in0=dist[c][:, j, :],
                 scalar=1.0,
                 in1=acc[:],
-                op0=ALU.min,
+                op0=ALU.subtract if signed else ALU.min,
                 op1=ALU.mult,
             )
 
@@ -205,30 +210,33 @@ def tile_kanlayer_t_kernel(tc, x, base_weight, spline_weight, grid, grad_out, ou
         def multiply(c):
             prod[c] = work.tile([P, HATS, CHUNK], F32, name="prod")
             if c != LAST_CHUNK:
-                pair[c] = terms_pool.tile([P, 2, CHUNK], F32, name="pair")
+                pair[c] = g_bf[c + 1][:].bitcast(F32).rearrange("p (a n) -> p a n", a=2)
             last[c] = terms_pool.tile([P, CHUNK], F32, name="last")
-            product(c, BASES)
-            product(c, 0)
-            product(c, 1)
-            product(c, 2)
-            if live(c - 1):
+            if c == LAST_CHUNK:
+                product(c, BASES)
+                acc = matmuls(c, "base")
+                nc.vector.tensor_tensor(out=last[c][:], in0=acc[:], in1=prod[c][:, BASES, :], op=ALU.add)
+                for j in range(BASES):
+                    product(c, j)
+                return
+            for j in range(BASES):
+                product(c, j)
+            if folded(c - 1):
                 fold(c - 1)
-            if live(c + X_AHEAD):
-                quantise(c + X_AHEAD)
-            product(c, 3)
-            if c != LAST_CHUNK:
-                nc.gpsimd.tensor_tensor(
-                    out=pair[c][:], in0=prod[c][:, 0:2, :], in1=prod[c][:, 2:4, :], op=ALU.add
-                )
+            quantise(c + X_AHEAD)
+            nc.gpsimd.tensor_tensor(
+                out=pair[c], in0=prod[c][:, 1:BASES:2, :], in1=prod[c][:, 0:BASES:2, :], op=ALU.subtract
+            )
+            product(c, BASES)
             acc = matmuls(c, "base")
-            nc.vector.tensor_tensor(out=last[c][:], in0=prod[c][:, BASES, :], in1=acc[:], op=ALU.add)
+            nc.vector.tensor_tensor(
+                out=last[c][:], in0=acc[:], in1=prod[c][:, BASES, :], op=ALU.subtract
+            )
 
         def turn_back(c):
             out_ps = psum_o.tile([P, TILES, IN_F], F32, name="out_ps")
             for t in range(TILES):
-                if c == LAST_CHUNK:
-                    terms = [prod[c][:, j, :] for j in range(BASES)] + [last[c][:]]
-                elif t < FOLDED:
+                if t < FOLDED and folded(c):
                     terms = [four[c][:], last[c][:]]
                 else:
                     terms = [pair[c][:, 0, :], pair[c][:, 1, :], last[c][:]]
@@ -245,13 +253,43 @@ def tile_kanlayer_t_kernel(tc, x, base_weight, spline_weight, grid, grad_out, ou
             nc.scalar.copy(out=out_sb[:], in_=out_ps[:])
             nc.sync.dma_start(out=out_rows[c], in_=out_sb[:].rearrange("p t i -> p (t i)"))
 
+        def turn_back_last(c):
+            banks = [psum_g.tile([P, 4, P], F32, name="g_t") for t in range(2)]
+            banks = [bank[:, 0, :] for bank in banks]
+            for t in range(2, TILES):
+                acc = psum_mx.tile([P, CHUNK], F32, name="acc")
+                banks.append(acc[:, 0:P])
+            terms = [last[c][:]] + [prod[c][:, j, :] for j in range(BASES)]
+            for n, term in enumerate(terms):
+                for t in range(TILES):
+                    nc.tensor.matmul(
+                        banks[t],
+                        lhsT=term[:, t * P : (t + 1) * P],
+                        rhs=ident[:],
+                        start=(n == 0),
+                        stop=(n == len(terms) - 1),
+                        is_transpose=True,
+                    )
+            out_sb = stores.tile([P, TILES, IN_F], F32, name="out_sb")
+            for t in range(2):
+                nc.scalar.copy(out=out_sb[:, t, :], in_=banks[t])
+                nc.vector.tensor_copy(out=out_sb[:, t + 2, :], in_=banks[t + 2])
+            half = 2 * IN_F
+            for h, queue in enumerate((nc.scalar, nc.sync)):
+                queue.dma_start(
+                    out=out_rows[c][:, h * half : (h + 1) * half],
+                    in_=out_sb[:, 2 * h : 2 * h + 2, :].rearrange("p t i -> p (t i)"),
+                )
+
         for c in range(LOOKAHEAD):
             load(c)
-        for i in range(-G_AHEAD, N_CHUNKS + BACK):
+        for i in range(-G_AHEAD, LAST_CHUNK + 1):
             if live(i + G_AHEAD + LOOKAHEAD):
                 load(i + G_AHEAD + LOOKAHEAD)
             if live(i - BACK):
                 turn_back(i - BACK)
+            if i == LAST_CHUNK:
+                turn_back(i - BACK + 1)
             if live(i + G_AHEAD):
                 turn_g(i + G_AHEAD)
             if live(i + X_AHEAD):
@@ -260,3 +298,6 @@ def tile_kanlayer_t_kernel(tc, x, base_weight, spline_weight, grid, grad_out, ou
                 multiply(i)
             elif live(i + X_AHEAD):
                 quantise(i + X_AHEAD)
+                prepare_base()
+        turn_back(LAST_CHUNK - 1)
+        turn_back_last(LAST_CHUNK)

@@ -28,6 +28,7 @@ BACK = 3
 LOOKAHEAD = 2
 FOLDED = 2
 
+PRODUCT_ORDER = (4, 0, 1, 2, 3)
 NEGATIVE = (0, 2, 4)
 
 FLOPS = 2 * TOKENS * OUT_F * (IN_F + IN_F * BASES)
@@ -153,7 +154,7 @@ def tile_kanlayer_t_kernel(tc, x, base_weight, spline_weight, grid, grad_out, ou
             for t in range(TILES):
                 nc.tensor.transpose(x_t[:, t * P : (t + 1) * P], x_sb[c][:, t, :], ident_bf[:])
             dist[c] = work3.tile([P, HATS, CHUNK], F32, name="dist")
-            for j in range(HATS):
+            for j in PRODUCT_ORDER:
                 nc.scalar.activation(
                     out=dist[c][:, j, :],
                     in_=x_t[:],
@@ -219,7 +220,7 @@ def tile_kanlayer_t_kernel(tc, x, base_weight, spline_weight, grid, grad_out, ou
                 for j in range(BASES):
                     product(c, j)
                 return
-            for j in range(BASES):
+            for j in PRODUCT_ORDER:
                 product(c, j)
             if folded(c - 1):
                 fold(c - 1)
@@ -227,7 +228,6 @@ def tile_kanlayer_t_kernel(tc, x, base_weight, spline_weight, grid, grad_out, ou
             nc.gpsimd.tensor_tensor(
                 out=pair[c], in0=prod[c][:, 1:BASES:2, :], in1=prod[c][:, 0:BASES:2, :], op=ALU.subtract
             )
-            product(c, BASES)
             acc = matmuls(c, "base")
             nc.vector.tensor_tensor(
                 out=last[c][:], in0=acc[:], in1=prod[c][:, BASES, :], op=ALU.subtract

@@ -150,9 +150,15 @@ def tile_kanlayer_t_kernel(tc, x, base_weight, spline_weight, grid, grad_out, ou
                 )
 
         def turn_x(c):
-            x_t = psum_x.tile([P, CHUNK], BF16, name="x_t")
+            x_t = psum_x.tile([P, CHUNK], F32, name="x_t")
             for t in range(TILES):
-                nc.tensor.transpose(x_t[:, t * P : (t + 1) * P], x_sb[c][:, t, :], ident_bf[:])
+                nc.tensor.matmul(
+                    x_t[:, t * P : (t + 1) * P],
+                    lhsT=x_sb[c][:, t, :],
+                    rhs=ident_bf[:],
+                    start=True,
+                    stop=True,
+                )
             dist[c] = work3.tile([P, HATS, CHUNK], F32, name="dist")
             for j in PRODUCT_ORDER:
                 nc.scalar.activation(

@@ -292,12 +292,12 @@ def tile_kanlayer_t_kernel(tc, x, base_weight, spline_weight, grid, grad_out, ou
         for i in range(-G_AHEAD, LAST_CHUNK + 1):
             if live(i + G_AHEAD + LOOKAHEAD):
                 load(i + G_AHEAD + LOOKAHEAD)
+            if live(i + G_AHEAD):
+                turn_g(i + G_AHEAD)
             if live(i - BACK):
                 turn_back(i - BACK)
             if i == LAST_CHUNK:
                 turn_back(i - BACK + 1)
-            if live(i + G_AHEAD):
-                turn_g(i + G_AHEAD)
             if live(i + X_AHEAD):
                 turn_x(i + X_AHEAD)
             if live(i):

@@ -23,6 +23,7 @@ CHUNK = P * TILES
 N_CHUNKS = TOKENS // CHUNK
 LAST_CHUNK = N_CHUNKS - 1
 G_AHEAD = 2
+Q_AHEAD = 2
 X_AHEAD = 1
 BACK = 3
 LOOKAHEAD = 2
@@ -42,6 +43,10 @@ def load_weight_rows(nc, raw, weight):
         )
 
 
+def quantised_in(i):
+    return [c for c in range(N_CHUNKS) if max(c - Q_AHEAD, min(c - 1, 0)) == i]
+
+
 def folded(c):
     return 0 <= c <= LAST_CHUNK - BACK
 
@@ -58,7 +63,7 @@ def tile_kanlayer_t_kernel(tc, x, base_weight, spline_weight, grid, grad_out, ou
         tc.tile_pool(name="loads_x", bufs=LOOKAHEAD + 2) as loads_x,
         tc.tile_pool(name="work", bufs=2) as work,
         tc.tile_pool(name="work3", bufs=3) as work3,
-        tc.tile_pool(name="shared", bufs=6) as shared,
+        tc.tile_pool(name="shared", bufs=7) as shared,
         tc.tile_pool(name="stores", bufs=N_CHUNKS) as stores,
         tc.tile_pool(name="terms", bufs=BACK) as terms_pool,
         tc.psum_pool(name="psum_g", bufs=2) as psum_g,
@@ -175,8 +180,8 @@ def tile_kanlayer_t_kernel(tc, x, base_weight, spline_weight, grid, grad_out, ou
                     )
 
         def quantise(c):
-            g_codes[c] = work.tile([P, CHUNK], U32, align_bytes=64, name="g_codes")
-            g_scales[c] = work.tile([P, CHUNK], U8, align_bytes=64, name="g_scales")
+            g_codes[c] = work3.tile([P, CHUNK], U32, align_bytes=64, name="g_codes")
+            g_scales[c] = work3.tile([P, CHUNK], U8, align_bytes=64, name="g_scales")
             nc.vector.quantize_mx(
                 out=g_codes[c][:].bitcast(E5M2_X4), scales=g_scales[c][:], in_=g_bf[c][:]
             )
@@ -217,7 +222,9 @@ def tile_kanlayer_t_kernel(tc, x, base_weight, spline_weight, grid, grad_out, ou
         def multiply(c):
             prod[c] = work.tile([P, HATS, CHUNK], F32, name="prod")
             if c != LAST_CHUNK:
-                pair[c] = g_bf[c + 1][:].bitcast(F32).rearrange("p (a n) -> p a n", a=2)
+                quantised = quantised_in(c)
+                spent = g_bf[quantised[-1]] if quantised else shared.tile([P, TILES * OUT_F], BF16, align_bytes=64, name="g_bf")
+                pair[c] = spent[:].bitcast(F32).rearrange("p (a n) -> p a n", a=2)
             last[c] = terms_pool.tile([P, CHUNK], F32, name="last")
             if c == LAST_CHUNK:
                 product(c, BASES)
@@ -230,7 +237,8 @@ def tile_kanlayer_t_kernel(tc, x, base_weight, spline_weight, grid, grad_out, ou
                 product(c, j)
             if folded(c - 1):
                 fold(c - 1)
-            quantise(c + X_AHEAD)
+            for q in quantised:
+                quantise(q)
             nc.gpsimd.tensor_tensor(
                 out=pair[c], in0=prod[c][:, 1:BASES:2, :], in1=prod[c][:, 0:BASES:2, :], op=ALU.subtract
             )
@@ -302,8 +310,8 @@ def tile_kanlayer_t_kernel(tc, x, base_weight, spline_weight, grid, grad_out, ou
                 turn_x(i + X_AHEAD)
             if live(i):
                 multiply(i)
-            elif live(i + X_AHEAD):
-                quantise(i + X_AHEAD)
+            for q in quantised_in(i) if i < 0 else []:
+                quantise(q)
                 prepare_base()
         turn_back(LAST_CHUNK - 1)
         turn_back_last(LAST_CHUNK)

import concourse.mybir as mybir
from concourse.masks import make_identity

F32 = mybir.dt.float32
BF16 = mybir.dt.bfloat16
U32 = mybir.dt.uint32
U8 = mybir.dt.uint8
E4M3_X4 = mybir.dt.float8_e4m3fn_x4
E5M2_X4 = mybir.dt.float8_e5m2_x4
ALU = mybir.AluOpType
ACT = mybir.ActivationFunctionType

P = 128
PACK = 4
TOKENS = 16384
OUT_F = 512
IN_F = 128
BASES = 4
HATS = BASES + 1
HALF = OUT_F // 2
TILES = 4
CHUNK = P * TILES
N_CHUNKS = TOKENS // CHUNK
LAST_CHUNK = N_CHUNKS - 1
G_AHEAD = 2
Q_AHEAD = 2
X_AHEAD = 1
BACK = 3
LOOKAHEAD = 2
FOLDED = 2

PRODUCT_ORDER = (4, 0, 1, 2, 3)
NEGATIVE = (0, 2, 4)

FLOPS = 2 * TOKENS * OUT_F * (IN_F + IN_F * BASES)


def load_weight_rows(nc, raw, weight):
    for u in range(2):
        nc.scalar.dma_start(
            out=raw[:, 2 * u : 2 * u + 2, :],
            in_=weight[HALF * u : HALF * (u + 1), :].rearrange("(p e) c -> p e c", e=2),
        )


def quantised_in(i):
    return [c for c in range(N_CHUNKS) if max(c - Q_AHEAD, min(c - 1, 0)) == i]


def folded(c):
    return 0 <= c <= LAST_CHUNK - BACK


def live(c):
    return 0 <= c < N_CHUNKS


def tile_kanlayer_t_kernel(tc, x, base_weight, spline_weight, grid, grad_out, out):
    nc = tc.nc
    with (
        tc.tile_pool(name="keep", bufs=1) as keep,
        tc.tile_pool(name="loads", bufs=LOOKAHEAD + 1) as loads,
        tc.tile_pool(name="loads_x", bufs=LOOKAHEAD + 2) as loads_x,
        tc.tile_pool(name="work", bufs=2) as work,
        tc.tile_pool(name="work3", bufs=3) as work3,
        tc.tile_pool(name="shared", bufs=7) as shared,
        tc.tile_pool(name="stores", bufs=N_CHUNKS) as stores,
        tc.tile_pool(name="terms", bufs=BACK) as terms_pool,
        tc.psum_pool(name="psum_g", bufs=2) as psum_g,
        tc.psum_pool(name="psum_x", bufs=1) as psum_x,
        tc.psum_pool(name="psum_o", bufs=1) as psum_o,
        tc.psum_pool(name="psum_mx", bufs=4) as psum_mx,
        tc.manual_schedule(),
    ):
        raw_sw = keep.tile([P, PACK, BASES * IN_F], BF16)
        load_weight_rows(nc, raw_sw, spline_weight.rearrange("o i l -> o (i l)"))
        raw_bw = keep.tile([P, PACK, IN_F], BF16)
        load_weight_rows(nc, raw_bw, base_weight)
        by_basis = raw_sw[:].rearrange("p k (i l) -> p l i k", l=BASES)

        signed_bf = keep.tile([P, BASES, IN_F, PACK], BF16, align_bytes=64)
        nc.vector.tensor_copy(out=signed_bf[:, 0:BASES:2], in_=by_basis[:, 0:BASES:2])
        nc.vector.tensor_scalar(
            out=signed_bf[:, 1:BASES:2],
            in0=by_basis[:, 1:BASES:2],
            scalar1=-1.0,
            scalar2=None,
            op0=ALU.mult,
        )
        sw_codes = keep.tile([P, BASES * IN_F], U32, align_bytes=64)
        sw_scales = keep.tile([P, BASES * IN_F], U8, align_bytes=64)
        nc.vector.quantize_mx(
            out=sw_codes[:].bitcast(E4M3_X4),
            scales=sw_scales[:],
            in_=signed_bf[:].rearrange("p a i k -> p (a i k)"),
        )
        bw_bf = keep.tile([P, IN_F, PACK], BF16, align_bytes=64)
        bw_codes = keep.tile([P, IN_F], U32, align_bytes=64)
        bw_scales = keep.tile([P, IN_F], U8, align_bytes=64)

        def prepare_base():
            nc.vector.tensor_copy(out=bw_bf[:], in_=raw_bw[:].rearrange("p k i -> p i k"))
            nc.vector.quantize_mx(
                out=bw_codes[:].bitcast(E4M3_X4),
                scales=bw_scales[:],
                in_=bw_bf[:].rearrange("p i k -> p (i k)"),
            )

        def plane(codes, scales, a):
            cols = slice(a * IN_F, (a + 1) * IN_F)
            return codes[:, cols].bitcast(E4M3_X4), scales[:, cols]

        passes_of = {"base": [plane(bw_codes, bw_scales, 0)]}
        for j in range(HATS):
            passes_of[j] = [plane(sw_codes, sw_scales, l) for l in (j - 1, j) if 0 <= l < BASES]

        ident = keep.tile([P, P], F32)
        make_identity(nc, ident[:])
        ident_bf = keep.tile([P, P], BF16)
        make_identity(nc, ident_bf[:])
        grid_bf = keep.tile([P, HATS + 2], BF16)
        nc.scalar.dma_start(out=grid_bf[:], in_=grid.partition_broadcast(P))
        minus_centre = keep.tile([P, HATS], F32)
        nc.gpsimd.tensor_scalar(
            out=minus_centre[:], in0=grid_bf[:, 1 : HATS + 1], scalar1=-1.0, scalar2=None, op0=ALU.mult
        )

        g_rows = grad_out.rearrange("(c p t) o -> c p (t o)", p=P, t=TILES)
        x_rows = x.rearrange("(c p t) i -> c p (t i)", p=P, t=TILES)
        out_rows = out.rearrange("(c p t) i -> c p (t i)", p=P, t=TILES)

        g_sb, x_sb, g_bf, g_codes, g_scales, dist, prod, pair, last, four = {}, {}, {}, {}, {}, {}, {}, {}, {}, {}

        def load(c):
            g_sb[c] = loads.tile([P, TILES * OUT_F], BF16, name="g_sb")
            nc.sync.dma_start(out=g_sb[c][:], in_=g_rows[c])
            x_sb[c] = loads_x.tile([P, TILES, IN_F], BF16, name="x_sb")
            nc.sync.dma_start(out=x_sb[c][:].rearrange("p t i -> p (t i)"), in_=x_rows[c])

        def turn_g(c):
            g_bf[c] = shared.tile([P, TILES * OUT_F], BF16, align_bytes=64, name="g_bf")
            g_words = g_sb[c][:].bitcast(F32)
            g_pairs = g_bf[c][:].bitcast(F32).rearrange("p (t r u) -> p t r u", r=P, u=2)
            for t in range(0, TILES, 2):
                g_t = psum_g.tile([P, 4, P], F32, name="g_t")
                for a in range(2):
                    for u in range(2):
                        first = ((t + a) * 2 + u) * P
                        nc.tensor.transpose(
                            g_t[:, 2 * a + u, :], g_words[:, first : first + P], ident[:]
                        )
                nc.scalar.copy(
                    out=g_pairs[:, t : t + 2, :, :],
                    in_=g_t[:].rearrange("p (a u) r -> p a r u", u=2),
                )

        def turn_x(c):
            x_t = psum_x.tile([P, CHUNK], F32, name="x_t")
            for t in range(TILES):
                nc.tensor.matmul(
                    x_t[:, t * P : (t + 1) * P],
                    lhsT=x_sb[c][:, t, :],
                    rhs=ident_bf[:],
                    start=True,
                    stop=True,
                )
            dist[c] = work3.tile([P, HATS, CHUNK], F32, name="dist")
            for j in PRODUCT_ORDER:
                nc.scalar.activation(
                    out=dist[c][:, j, :],
                    in_=x_t[:],
                    func=ACT.Abs,
                    bias=minus_centre[:, j : j + 1],
                    scale=1.0,
                )
            if c == LAST_CHUNK:
                for j in NEGATIVE:
                    nc.scalar.activation(
                        out=dist[c][:, j, :], in_=dist[c][:, j, :], func=ACT.Relu, bias=1.0, scale=-1.0
                    )

        def quantise(c):
            g_codes[c] = work3.tile([P, CHUNK], U32, align_bytes=64, name="g_codes")
            g_scales[c] = work3.tile([P, CHUNK], U8, align_bytes=64, name="g_scales")
            nc.vector.quantize_mx(
                out=g_codes[c][:].bitcast(E5M2_X4), scales=g_scales[c][:], in_=g_bf[c][:]
            )

        def matmuls(c, which):
            acc = psum_mx.tile([P, CHUNK], F32, name="acc")
            passes = passes_of[which]
            for n, (codes, scales) in enumerate(passes):
                nc.tensor.matmul_mx(
                    out=acc[:],
                    lhsT=codes,
                    lhsT_scale=scales,
                    rhs=g_codes[c][:].bitcast(E5M2_X4),
                    rhs_scale=g_scales[c][:],
                    start=(n == 0),
                    stop=(n == len(passes) - 1),
                )
            return acc

        def product(c, j):
            acc = matmuls(c, j)
            signed = c == LAST_CHUNK and j in NEGATIVE
            nc.vector.scalar_tensor_tensor(
                out=prod[c][:, j, :],
                in0=dist[c][:, j, :],
                scalar=1.0,
                in1=acc[:],
                op0=ALU.subtract if signed else ALU.min,
                op1=ALU.mult,
            )

        def fold(c):
            four[c] = work.tile([P, FOLDED * P], F32, name="four")
            nc.vector.tensor_tensor(
                out=four[c][:], in0=pair[c][:, 0, 0 : FOLDED * P], in1=pair[c][:, 1, 0 : FOLDED * P], op=ALU.add
            )

        def multiply(c):
            prod[c] = work.tile([P, HATS, CHUNK], F32, name="prod")
            if c != LAST_CHUNK:
                quantised = quantised_in(c)
                spent = g_bf[quantised[-1]] if quantised else shared.tile([P, TILES * OUT_F], BF16, align_bytes=64, name="g_bf")
                pair[c] = spent[:].bitcast(F32).rearrange("p (a n) -> p a n", a=2)
            last[c] = terms_pool.tile([P, CHUNK], F32, name="last")
            if c == LAST_CHUNK:
                product(c, BASES)
                acc = matmuls(c, "base")
                nc.vector.tensor_tensor(out=last[c][:], in0=acc[:], in1=prod[c][:, BASES, :], op=ALU.add)
                for j in range(BASES):
                    product(c, j)
                return
            for j in PRODUCT_ORDER:
                product(c, j)
            if folded(c - 1):
                fold(c - 1)
            for q in quantised:
                quantise(q)
            nc.gpsimd.tensor_tensor(
                out=pair[c], in0=prod[c][:, 1:BASES:2, :], in1=prod[c][:, 0:BASES:2, :], op=ALU.subtract
            )
            acc = matmuls(c, "base")
            nc.vector.tensor_tensor(
                out=last[c][:], in0=acc[:], in1=prod[c][:, BASES, :], op=ALU.subtract
            )

        def turn_back(c):
            out_ps = psum_o.tile([P, TILES, IN_F], F32, name="out_ps")
            for t in range(TILES):
                if t < FOLDED and folded(c):
                    terms = [four[c][:], last[c][:]]
                else:
                    terms = [pair[c][:, 0, :], pair[c][:, 1, :], last[c][:]]
                for n, term in enumerate(terms):
                    nc.tensor.matmul(
                        out_ps[:, t, :],
                        lhsT=term[:, t * P : (t + 1) * P],
                        rhs=ident[:],
                        start=(n == 0),
                        stop=(n == len(terms) - 1),
                        is_transpose=True,
                    )
            out_sb = stores.tile([P, TILES, IN_F], F32, name="out_sb")
            nc.scalar.copy(out=out_sb[:], in_=out_ps[:])
            nc.sync.dma_start(out=out_rows[c], in_=out_sb[:].rearrange("p t i -> p (t i)"))

        def turn_back_last(c):
            banks = [psum_g.tile([P, 4, P], F32, name="g_t") for t in range(2)]
            banks = [bank[:, 0, :] for bank in banks]
            for t in range(2, TILES):
                acc = psum_mx.tile([P, CHUNK], F32, name="acc")
                banks.append(acc[:, 0:P])
            terms = [last[c][:]] + [prod[c][:, j, :] for j in range(BASES)]
            for n, term in enumerate(terms):
                for t in range(TILES):
                    nc.tensor.matmul(
                        banks[t],
                        lhsT=term[:, t * P : (t + 1) * P],
                        rhs=ident[:],
                        start=(n == 0),
                        stop=(n == len(terms) - 1),
                        is_transpose=True,
                    )
            out_sb = stores.tile([P, TILES, IN_F], F32, name="out_sb")
            for t in range(2):
                nc.scalar.copy(out=out_sb[:, t, :], in_=banks[t])
                nc.vector.tensor_copy(out=out_sb[:, t + 2, :], in_=banks[t + 2])
            half = 2 * IN_F
            for h, queue in enumerate((nc.scalar, nc.sync)):
                queue.dma_start(
                    out=out_rows[c][:, h * half : (h + 1) * half],
                    in_=out_sb[:, 2 * h : 2 * h + 2, :].rearrange("p t i -> p (t i)"),
                )

        for c in range(LOOKAHEAD):
            load(c)
        for i in range(-G_AHEAD, LAST_CHUNK + 1):
            if live(i + G_AHEAD + LOOKAHEAD):
                load(i + G_AHEAD + LOOKAHEAD)
            if live(i + G_AHEAD):
                turn_g(i + G_AHEAD)
            if live(i - BACK):
                turn_back(i - BACK)
            if i == LAST_CHUNK:
                turn_back(i - BACK + 1)
            if live(i + X_AHEAD):
                turn_x(i + X_AHEAD)
            if live(i):
                multiply(i)
            for q in quantised_in(i) if i < 0 else []:
                quantise(q)
                prepare_base()
        turn_back(LAST_CHUNK - 1)
        turn_back_last(LAST_CHUNK)
